import numpy as np
import ml_dtypes


def mxq(x, axis, fmt="e4m3"):
    dtype, down = {"e4m3": (ml_dtypes.float8_e4m3fn, 7), "e5m2": (ml_dtypes.float8_e5m2, 14)}[fmt]
    v = np.moveaxis(np.asarray(x, np.float32).astype(ml_dtypes.bfloat16).astype(np.float64), axis, -1)
    blocks = v.reshape(v.shape[:-1] + (-1, 32))
    amax = np.abs(blocks).max(-1, keepdims=True)
    byte = np.maximum(np.where(amax > 0, np.frexp(amax)[1] - 1 + 127, 0) - down, 1)
    scale = np.exp2(byte - 127.0)
    codes = (blocks / scale).astype(np.float32).astype(dtype).astype(np.float64)
    return np.moveaxis((codes * scale).reshape(v.shape), -1, axis)


WIDE = False


def mx_kscale(k):
    if not WIDE:
        return np.ones(k)
    levels = np.array([10, -10, 5, -5, 0])
    if k % 512:
        return np.exp2(np.random.permutation(np.resize(levels, k // 32))).repeat(32)
    a = np.empty((k // 512, 16))
    for p in range(k // 512):
        a[p, :8] = np.random.permutation(np.resize(levels, 8))
        for g in range(8):
            far = levels[np.abs(levels - a[p, g]) >= 10]
            a[p, g + 8] = far[np.random.randint(len(far))]
    return np.exp2(a.ravel()).repeat(32)


BF16 = ml_dtypes.bfloat16


def bf(x):
    return np.asarray(x, np.float32).astype(BF16)


def f64(x):
    return np.asarray(x).astype(np.float64)


B, S, NI, NO = 4, 576, 128, 128


def setup_inputs():
    sn = mx_kscale(4 * NI)[::4]
    sc = NI ** -0.5

    def u():
        return bf(np.random.uniform(-sc, sc, (NO, NI)) / sn[None, :])

    return {"q_in": bf(np.random.standard_normal((B, S, 4 * NI)) * np.repeat(sn, 4)),
            "r_weight": u(), "i_weight": u(), "j_weight": u(), "k_weight": u()}


def reference(q_in, r_weight, i_weight, j_weight, k_weight):
    q = f64(q_in)
    V = np.stack([f64(r_weight), f64(i_weight), f64(j_weight), f64(k_weight)]).transpose(2, 0, 1).reshape(4 * NI, NO)
    Vq = mxq(V, 0, "e4m3")
    Wr, Wi, Wj, Wk = Vq.reshape(NI, 4, NO).transpose(1, 2, 0)
    W4 = np.stack([
        np.stack([Wr, -Wi, -Wj, -Wk]),
        np.stack([Wi, Wr, Wk, -Wj]),
        np.stack([Wj, -Wk, Wr, Wi]),
        np.stack([Wk, Wj, -Wi, Wr]),
    ])
    W = W4.transpose(3, 1, 2, 0).reshape(4 * NI, 4 * NO)
    return mxq(q, 2, "e4m3") @ W

@@ -1,0 +1,249 @@
+from contextlib import ExitStack
+
+import concourse.mybir as mybir
+from concourse.masks import make_identity
+
+F32 = mybir.dt.float32
+BF16 = mybir.dt.bfloat16
+U32 = mybir.dt.uint32
+U8 = mybir.dt.uint8
+FP8X4 = mybir.dt.float8_e4m3fn_x4
+MULT = mybir.AluOpType.mult
+ADD = mybir.AluOpType.add
+
+P = 128
+TOKENS = 4 * 576
+K = 512
+N_OUT = 512
+TILES = TOKENS // P
+FLOPS = 2 * TOKENS * K * N_OUT
+
+LOAD_CHUNKS = (1, 3, 4, 4, 6)
+GROUPS = ((0,), (1,)) + tuple((t, t + 1) for t in range(2, TILES, 2))
+STORES = ((0,), (1,)) + tuple((t, t + 1) for t in range(2, TILES - 2, 2)) + ((TILES - 2,), (TILES - 1,))
+LEAD = 2
+
+
+def tile_quaternionlinear_kernel(tc, q_in, r_weight, i_weight, j_weight, k_weight, out):
+    nc = tc.nc
+    q_view = q_in.flatten_outer_dims().rearrange("(p t) k -> p t k", t=TILES)
+    out_view = out.flatten_outer_dims().rearrange("(p t) c -> p t c", t=TILES)
+
+    def copy(engine, dst, src):
+        if engine == "V":
+            nc.vector.tensor_copy(out=dst, in_=src)
+        else:
+            nc.scalar.copy(out=dst, in_=src)
+
+    with ExitStack() as ctx:
+        keep = ctx.enter_context(tc.tile_pool(name="keep", bufs=1))
+        psum_t = ctx.enter_context(tc.psum_pool(name="psum_t", bufs=2))
+        psum_w = ctx.enter_context(tc.psum_pool(name="psum_w", bufs=1))
+        psum_o = ctx.enter_context(tc.psum_pool(name="psum_o", bufs=5))
+        ctx.enter_context(tc.manual_schedule())
+
+        planes = keep.tile([P, 9, P], BF16, name="planes")
+        nc.sync.dma_start(out=planes[:, 0:9:8, :], in_=i_weight.unsqueeze(1).to_broadcast([P, 2, P]))
+        nc.sync.dma_start(out=planes[:, 2, :], in_=k_weight)
+        nc.sync.dma_start(out=planes[:, 5, :], in_=j_weight)
+        nc.sync.dma_start(out=planes[:, 1:8:6, :], in_=r_weight.unsqueeze(1).to_broadcast([P, 2, P]))
+
+        q_tiles = []
+        first = 0
+        for ci, count in enumerate(LOAD_CHUNKS):
+            q_chunk = keep.tile([P, count, K], BF16, name="q_chunk%d" % ci)
+            nc.sync.dma_start(out=q_chunk[:], in_=q_view[:, first : first + count, :])
+            for j in range(count):
+                q_tiles.append(q_chunk[:, j, :])
+            first += count
+
+        ident = keep.tile([P, P], F32, name="ident")
+        make_identity(nc, ident[:])
+
+        signed = keep.tile([P, 4, P, 4], BF16, name="signed")
+        signed_words = signed[:].rearrange("p d n c -> p (d n c)").bitcast(F32)
+        w_codes = keep.tile([P, N_OUT], U32, name="w_codes", align_bytes=64)
+        w_scales = keep.tile([P, N_OUT], U8, name="w_scales", align_bytes=64)
+        w_banks = {}
+        w_grouped = {}
+
+        def plane_grid(d):
+            if d == 1:
+                return planes[:, 0:4, :].rearrange("p (b e) n -> p n b e", e=2)
+            if d == 2:
+                return planes[:, 5:9, :].rearrange("p (b e) n -> p n b e", e=2)
+            base = 1 if d == 0 else 2
+            six = planes[:, base : base + 6, :].rearrange("p (e x) n -> p e x n", x=3)
+            return six[:, :, 0:3:2, :].rearrange("p e b n -> p n b e")
+
+        def negate_i_and_k():
+            nc.vector.tensor_scalar_mul(out=planes[:, 4:7:2, :], in0=planes[:, 0:3:2, :], scalar1=-1.0)
+
+        def negate_j():
+            nc.gpsimd.tensor_scalar(out=planes[:, 3, :], in0=planes[:, 5, :], scalar1=-1.0, scalar2=0.0, op0=MULT, op1=ADD)
+
+        def regroup(d):
+            engine = "S" if d == 1 else "V"
+            copy(engine, signed[:, d, :, :].rearrange("p n (b e) -> p n b e", e=2), plane_grid(d))
+
+        def transpose_weights(d):
+            tw = psum_o.tile([P, 2, P], F32, tag="o", name="tw%d" % d)
+            for u in range(2):
+                col = 2 * d * P
+                nc.tensor.transpose(tw[:, u, :], signed_words[:, col + u : col + 2 * P : 2], ident[:])
+            w_banks[d] = tw
+
+        def copy_weights(d):
+            wg = keep.tile([P, 4 * P], BF16, name="w_grouped%d" % d, align_bytes=64)
+            engine = "V" if d == 0 else "S"
+            copy(engine, wg[:].bitcast(F32).rearrange("p (m u) -> p m u", u=2), w_banks[d][:].rearrange("p u m -> p m u"))
+            w_grouped[d] = wg
+
+        def quantise_weights(d):
+            cols = slice(d * P, (d + 1) * P)
+            nc.vector.quantize_mx(out=w_codes[:, cols].bitcast(FP8X4), scales=w_scales[:, cols], in_=w_grouped[d][:])
+
+        q_banks = {}
+        q_grouped = {}
+        q_codes = {}
+        q_scales = {}
+        slot_of = {}
+        for g, tiles in enumerate(GROUPS):
+            for s, t in enumerate(tiles):
+                slot_of[t] = (g, s)
+
+        def transpose_tokens(g):
+            count = len(GROUPS[g])
+            tq = psum_t.tile([P, count, 2, P], F32, tag="t", name="tq%d" % g)
+            for s, t in enumerate(GROUPS[g]):
+                words = q_tiles[t].bitcast(F32)
+                for u in range(2):
+                    nc.tensor.transpose(tq[:, s, u, :], words[:, u : 2 * P : 2], ident[:])
+            q_banks[g] = tq
+
+        def copy_tokens(g):
+            count = len(GROUPS[g])
+            grouped = keep.tile([P, count * 4 * P], BF16, name="grouped%d" % g, align_bytes=64)
+            copy(
+                "S" if g < 3 else "V",
+                grouped[:].bitcast(F32).rearrange("p (s k u) -> p s k u", s=count, u=2),
+                q_banks[g][:].rearrange("p s u k -> p s k u"),
+            )
+            q_grouped[g] = grouped
+
+        def quantise_tokens(g):
+            count = len(GROUPS[g])
+            codes = keep.tile([P, count * P], U32, name="codes%d" % g, align_bytes=64)
+            scales = keep.tile([P, count * P], U8, name="scales%d" % g, align_bytes=64)
+            nc.vector.quantize_mx(out=codes[:].bitcast(FP8X4), scales=scales[:], in_=q_grouped[g][:])
+            q_codes[g] = codes
+            q_scales[g] = scales
+
+        def prepare(g):
+            transpose_tokens(g)
+            copy_tokens(g)
+            quantise_tokens(g)
+
+        store_of = {}
+        store_rows = {}
+        left = {}
+        for si, tiles in enumerate(STORES):
+            left[si] = len(tiles)
+            for s, t in enumerate(tiles):
+                store_of[t] = (si, s)
+
+        accs = {}
+        warm_bank = psum_w.tile([P, P], F32, name="warm_bank")
+
+        def warm(count):
+            for r in range(count):
+                nc.tensor.matmul(out=warm_bank[:], lhsT=ident[:], rhs=ident[:], start=True, stop=True)
+
+        def multiply(t):
+            g, s = slot_of[t]
+            acc = psum_o.tile([P, N_OUT], F32, tag="o", name="acc%d" % t)
+            nc.tensor.matmul_mx(
+                out=acc[:],
+                lhsT=q_codes[g][:, s * P : (s + 1) * P].bitcast(FP8X4),
+                lhsT_scale=q_scales[g][:, s * P : (s + 1) * P],
+                rhs=w_codes[:].bitcast(FP8X4),
+                rhs_scale=w_scales[:],
+                start=True,
+                stop=True,
+            )
+            accs[t] = acc
+
+        def multiply_component(d):
+            g, s = slot_of[0]
+            if 0 not in accs:
+                accs[0] = psum_o.tile([P, N_OUT], F32, tag="o", name="acc0")
+            cols = slice(d * P, (d + 1) * P)
+            nc.tensor.matmul_mx(
+                out=accs[0][:, cols],
+                lhsT=q_codes[g][:, s * P : (s + 1) * P].bitcast(FP8X4),
+                lhsT_scale=q_scales[g][:, s * P : (s + 1) * P],
+                rhs=w_codes[:, cols].bitcast(FP8X4),
+                rhs_scale=w_scales[:, cols],
+                start=True,
+                stop=True,
+            )
+
+        def copy_out(t):
+            si, ss = store_of[t]
+            if si not in store_rows:
+                store_rows[si] = keep.tile([P, len(STORES[si]), N_OUT], F32, name="o_sb%d" % si)
+            copy(
+                "V" if t >= TILES - 5 and t % 2 == 1 else "S",
+                store_rows[si][:, ss, :].rearrange("p (m d) -> p m d", d=4),
+                accs[t][:].rearrange("p (d m) -> p m d", d=4),
+            )
+            left[si] -= 1
+            if left[si] == 0:
+                t0 = STORES[si][0]
+                nc.sync.dma_start(out=out_view[:, t0 : t0 + len(STORES[si]), :], in_=store_rows[si][:])
+
+        warm(5)
+        negate_i_and_k()
+        negate_j()
+        regroup(3)
+        regroup(1)
+        transpose_tokens(0)
+        warm(1)
+        regroup(2)
+        transpose_weights(3)
+        warm(1)
+        copy_tokens(0)
+        regroup(0)
+        transpose_weights(2)
+        copy_weights(3)
+        quantise_tokens(0)
+        transpose_weights(1)
+        warm(1)
+        copy_weights(2)
+        quantise_weights(3)
+        transpose_weights(0)
+        copy_weights(1)
+        quantise_weights(2)
+        transpose_tokens(1)
+        copy_weights(0)
+        quantise_weights(1)
+        quantise_weights(0)
+        copy_tokens(1)
+        quantise_tokens(1)
+        transpose_tokens(2)
+        warm(1)
+        copy_tokens(2)
+        quantise_tokens(2)
+        prepare(3)
+        for d in (3, 2, 1, 0):
+            multiply_component(d)
+        copy_out(0)
+        multiply(1)
+        copy_out(1)
+        for g in range(2, len(GROUPS), 2):
+            for h in (g + LEAD, g + LEAD + 1):
+                if h < len(GROUPS):
+                    prepare(h)
+            for t in GROUPS[g] + GROUPS[g + 1]:
+                multiply(t)
+                copy_out(t)

@@ -8,8 +8,6 @@ BF16 = mybir.dt.bfloat16
 U32 = mybir.dt.uint32
 U8 = mybir.dt.uint8
 FP8X4 = mybir.dt.float8_e4m3fn_x4
-MULT = mybir.AluOpType.mult
-ADD = mybir.AluOpType.add
 
 P = 128
 TOKENS = 4 * 576
@@ -18,10 +16,12 @@ N_OUT = 512
 TILES = TOKENS // P
 FLOPS = 2 * TOKENS * K * N_OUT
 
+SIGN = ((1, -1, -1, -1), (1, 1, 1, -1), (1, -1, 1, 1), (1, 1, -1, 1))
+COMPONENTS = (3, 2, 1, 0)
+
 LOAD_CHUNKS = (1, 3, 4, 4, 6)
 GROUPS = ((0,), (1,)) + tuple((t, t + 1) for t in range(2, TILES, 2))
 STORES = ((0,), (1,)) + tuple((t, t + 1) for t in range(2, TILES - 2, 2)) + ((TILES - 2,), (TILES - 1,))
-LEAD = 2
 
 
 def tile_quaternionlinear_kernel(tc, q_in, r_weight, i_weight, j_weight, k_weight, out):
@@ -37,16 +37,15 @@ def tile_quaternionlinear_kernel(tc, q_in, r_weight, i_weight, j_weight, k_weigh
 
     with ExitStack() as ctx:
         keep = ctx.enter_context(tc.tile_pool(name="keep", bufs=1))
-        psum_t = ctx.enter_context(tc.psum_pool(name="psum_t", bufs=2))
-        psum_w = ctx.enter_context(tc.psum_pool(name="psum_w", bufs=1))
+        psum_t = ctx.enter_context(tc.psum_pool(name="psum_t", bufs=3))
         psum_o = ctx.enter_context(tc.psum_pool(name="psum_o", bufs=5))
         ctx.enter_context(tc.manual_schedule())
 
-        planes = keep.tile([P, 9, P], BF16, name="planes")
-        nc.sync.dma_start(out=planes[:, 0:9:8, :], in_=i_weight.unsqueeze(1).to_broadcast([P, 2, P]))
-        nc.sync.dma_start(out=planes[:, 2, :], in_=k_weight)
-        nc.sync.dma_start(out=planes[:, 5, :], in_=j_weight)
-        nc.sync.dma_start(out=planes[:, 1:8:6, :], in_=r_weight.unsqueeze(1).to_broadcast([P, 2, P]))
+        weights = []
+        for name, weight in (("w_r", r_weight), ("w_i", i_weight), ("w_j", j_weight), ("w_k", k_weight)):
+            w_sb = keep.tile([P, P], BF16, name=name)
+            nc.sync.dma_start(out=w_sb[:], in_=weight)
+            weights.append(w_sb)
 
         q_tiles = []
         first = 0
@@ -57,46 +56,43 @@ def tile_quaternionlinear_kernel(tc, q_in, r_weight, i_weight, j_weight, k_weigh
                 q_tiles.append(q_chunk[:, j, :])
             first += count
 
+        zeros = keep.tile([P, P], F32, name="zeros")
+        nc.vector.memset(zeros[:], 0.0)
+        scratch = keep.tile([P, 1], F32, name="scratch")
+        nc.scalar.copy(out=scratch[:], in_=zeros[:, 0:1])
+        warm_bank = psum_o.tile([P, P], F32, tag="o", name="warm_bank")
+        for r in range(5):
+            nc.tensor.matmul(out=warm_bank[:], lhsT=zeros[:], rhs=zeros[:], start=True, stop=True)
+
         ident = keep.tile([P, P], F32, name="ident")
         make_identity(nc, ident[:])
+        plus = keep.tile([P, P], BF16, name="plus")
+        minus = keep.tile([P, P], BF16, name="minus")
+        nc.vector.tensor_copy(out=plus[:], in_=ident[:])
+        nc.vector.tensor_scalar_mul(out=minus[:], in0=ident[:], scalar1=-1.0)
 
-        signed = keep.tile([P, 4, P, 4], BF16, name="signed")
-        signed_words = signed[:].rearrange("p d n c -> p (d n c)").bitcast(F32)
         w_codes = keep.tile([P, N_OUT], U32, name="w_codes", align_bytes=64)
         w_scales = keep.tile([P, N_OUT], U8, name="w_scales", align_bytes=64)
         w_banks = {}
+        for d in COMPONENTS:
+            w_banks[d] = psum_o.tile([P, 4, P], F32, tag="o", name="w_bank%d" % d)
         w_grouped = {}
 
-        def plane_grid(d):
-            if d == 1:
-                return planes[:, 0:4, :].rearrange("p (b e) n -> p n b e", e=2)
-            if d == 2:
-                return planes[:, 5:9, :].rearrange("p (b e) n -> p n b e", e=2)
-            base = 1 if d == 0 else 2
-            six = planes[:, base : base + 6, :].rearrange("p (e x) n -> p e x n", x=3)
-            return six[:, :, 0:3:2, :].rearrange("p e b n -> p n b e")
+        def transpose_weights():
+            for w in range(4):
+                for d in COMPONENTS:
+                    c = d ^ w
+                    nc.tensor.matmul(
+                        out=w_banks[d][:, c, :],
+                        lhsT=weights[w][:],
+                        rhs=plus[:] if SIGN[d][c] > 0 else minus[:],
+                        start=True,
+                        stop=True,
+                    )
 
-        def negate_i_and_k():
-            nc.vector.tensor_scalar_mul(out=planes[:, 4:7:2, :], in0=planes[:, 0:3:2, :], scalar1=-1.0)
-
-        def negate_j():
-            nc.gpsimd.tensor_scalar(out=planes[:, 3, :], in0=planes[:, 5, :], scalar1=-1.0, scalar2=0.0, op0=MULT, op1=ADD)
-
-        def regroup(d):
-            engine = "S" if d == 1 else "V"
-            copy(engine, signed[:, d, :, :].rearrange("p n (b e) -> p n b e", e=2), plane_grid(d))
-
-        def transpose_weights(d):
-            tw = psum_o.tile([P, 2, P], F32, tag="o", name="tw%d" % d)
-            for u in range(2):
-                col = 2 * d * P
-                nc.tensor.transpose(tw[:, u, :], signed_words[:, col + u : col + 2 * P : 2], ident[:])
-            w_banks[d] = tw
-
-        def copy_weights(d):
+        def copy_weights(engine, d):
             wg = keep.tile([P, 4 * P], BF16, name="w_grouped%d" % d, align_bytes=64)
-            engine = "V" if d == 0 else "S"
-            copy(engine, wg[:].bitcast(F32).rearrange("p (m u) -> p m u", u=2), w_banks[d][:].rearrange("p u m -> p m u"))
+            copy(engine, wg[:].rearrange("p (m c) -> p m c", c=4), w_banks[d][:].rearrange("p c m -> p m c"))
             w_grouped[d] = wg
 
         def quantise_weights(d):
@@ -121,11 +117,11 @@ def tile_quaternionlinear_kernel(tc, q_in, r_weight, i_weight, j_weight, k_weigh
                     nc.tensor.transpose(tq[:, s, u, :], words[:, u : 2 * P : 2], ident[:])
             q_banks[g] = tq
 
-        def copy_tokens(g):
+        def copy_tokens(engine, g):
             count = len(GROUPS[g])
             grouped = keep.tile([P, count * 4 * P], BF16, name="grouped%d" % g, align_bytes=64)
             copy(
-                "S" if g < 3 else "V",
+                engine,
                 grouped[:].bitcast(F32).rearrange("p (s k u) -> p s k u", s=count, u=2),
                 q_banks[g][:].rearrange("p s u k -> p s k u"),
             )
@@ -139,11 +135,6 @@ def tile_quaternionlinear_kernel(tc, q_in, r_weight, i_weight, j_weight, k_weigh
             q_codes[g] = codes
             q_scales[g] = scales
 
-        def prepare(g):
-            transpose_tokens(g)
-            copy_tokens(g)
-            quantise_tokens(g)
-
         store_of = {}
         store_rows = {}
         left = {}
@@ -151,13 +142,6 @@ def tile_quaternionlinear_kernel(tc, q_in, r_weight, i_weight, j_weight, k_weigh
             left[si] = len(tiles)
             for s, t in enumerate(tiles):
                 store_of[t] = (si, s)
-
-        accs = {}
-        warm_bank = psum_w.tile([P, P], F32, name="warm_bank")
-
-        def warm(count):
-            for r in range(count):
-                nc.tensor.matmul(out=warm_bank[:], lhsT=ident[:], rhs=ident[:], start=True, stop=True)
 
         def multiply(t):
             g, s = slot_of[t]
@@ -171,79 +155,44 @@ def tile_quaternionlinear_kernel(tc, q_in, r_weight, i_weight, j_weight, k_weigh
                 start=True,
                 stop=True,
             )
-            accs[t] = acc
-
-        def multiply_component(d):
-            g, s = slot_of[0]
-            if 0 not in accs:
-                accs[0] = psum_o.tile([P, N_OUT], F32, tag="o", name="acc0")
-            cols = slice(d * P, (d + 1) * P)
-            nc.tensor.matmul_mx(
-                out=accs[0][:, cols],
-                lhsT=q_codes[g][:, s * P : (s + 1) * P].bitcast(FP8X4),
-                lhsT_scale=q_scales[g][:, s * P : (s + 1) * P],
-                rhs=w_codes[:, cols].bitcast(FP8X4),
-                rhs_scale=w_scales[:, cols],
-                start=True,
-                stop=True,
-            )
-
-        def copy_out(t):
             si, ss = store_of[t]
             if si not in store_rows:
                 store_rows[si] = keep.tile([P, len(STORES[si]), N_OUT], F32, name="o_sb%d" % si)
             copy(
                 "V" if t >= TILES - 5 and t % 2 == 1 else "S",
                 store_rows[si][:, ss, :].rearrange("p (m d) -> p m d", d=4),
-                accs[t][:].rearrange("p (d m) -> p m d", d=4),
+                acc[:].rearrange("p (d m) -> p m d", d=4),
             )
             left[si] -= 1
             if left[si] == 0:
                 t0 = STORES[si][0]
                 nc.sync.dma_start(out=out_view[:, t0 : t0 + len(STORES[si]), :], in_=store_rows[si][:])
 
-        warm(5)
-        negate_i_and_k()
-        negate_j()
-        regroup(3)
-        regroup(1)
+        transpose_weights()
         transpose_tokens(0)
-        warm(1)
-        regroup(2)
-        transpose_weights(3)
-        warm(1)
-        copy_tokens(0)
-        regroup(0)
-        transpose_weights(2)
-        copy_weights(3)
-        quantise_tokens(0)
-        transpose_weights(1)
-        warm(1)
-        copy_weights(2)
-        quantise_weights(3)
-        transpose_weights(0)
-        copy_weights(1)
-        quantise_weights(2)
         transpose_tokens(1)
-        copy_weights(0)
-        quantise_weights(1)
-        quantise_weights(0)
-        copy_tokens(1)
-        quantise_tokens(1)
+        copy_weights("V", 3)
+        copy_weights("S", 2)
+        copy_weights("V", 1)
+        copy_weights("S", 0)
+        copy_tokens("S", 0)
+        copy_tokens("S", 1)
+        for d in COMPONENTS:
+            quantise_weights(d)
+        quantise_tokens(0)
         transpose_tokens(2)
-        warm(1)
-        copy_tokens(2)
+        copy_tokens("V", 2)
+        quantise_tokens(1)
         quantise_tokens(2)
-        prepare(3)
-        for d in (3, 2, 1, 0):
-            multiply_component(d)
-        copy_out(0)
+        multiply(0)
         multiply(1)
-        copy_out(1)
-        for g in range(2, len(GROUPS), 2):
-            for h in (g + LEAD, g + LEAD + 1):
-                if h < len(GROUPS):
-                    prepare(h)
-            for t in GROUPS[g] + GROUPS[g + 1]:
-                multiply(t)
-                copy_out(t)
+        for prepared, multiplied in (((3, 4), (2,)), ((5, 6), (3, 4)), ((7, 8), (5, 6)), ((9,), (7, 8, 9))):
+            for g in prepared:
+                transpose_tokens(g)
+            for g in prepared:
+                copy_tokens("V", g)
+            for g in prepared:
+                quantise_tokens(g)
+            for g in multiplied:
+                for t in GROUPS[g]:
+                    multiply(t)

@@ -21,6 +21,7 @@ COMPONENTS = (3, 2, 1, 0)
 
 LOAD_CHUNKS = (1, 3, 4, 4, 6)
 GROUPS = ((0,), (1,)) + tuple((t, t + 1) for t in range(2, TILES, 2))
+VECTOR_TILES = (11, 15, 17)
 STORES = ((0,), (1,)) + tuple((t, t + 1) for t in range(2, TILES - 2, 2)) + ((TILES - 2,), (TILES - 1,))
 
 
@@ -38,7 +39,8 @@ def tile_quaternionlinear_kernel(tc, q_in, r_weight, i_weight, j_weight, k_weigh
     with ExitStack() as ctx:
         keep = ctx.enter_context(tc.tile_pool(name="keep", bufs=1))
         psum_t = ctx.enter_context(tc.psum_pool(name="psum_t", bufs=3))
-        psum_o = ctx.enter_context(tc.psum_pool(name="psum_o", bufs=5))
+        psum_w = ctx.enter_context(tc.psum_pool(name="psum_w", bufs=1))
+        psum_o = ctx.enter_context(tc.psum_pool(name="psum_o", bufs=4))
         ctx.enter_context(tc.manual_schedule())
 
         weights = []
@@ -60,9 +62,13 @@ def tile_quaternionlinear_kernel(tc, q_in, r_weight, i_weight, j_weight, k_weigh
         nc.vector.memset(zeros[:], 0.0)
         scratch = keep.tile([P, 1], F32, name="scratch")
         nc.scalar.copy(out=scratch[:], in_=zeros[:, 0:1])
-        warm_bank = psum_o.tile([P, P], F32, tag="o", name="warm_bank")
-        for r in range(5):
-            nc.tensor.matmul(out=warm_bank[:], lhsT=zeros[:], rhs=zeros[:], start=True, stop=True)
+        warm_bank = psum_w.tile([P, P], F32, name="warm_bank")
+
+        def warm(count):
+            for r in range(count):
+                nc.tensor.matmul(out=warm_bank[:], lhsT=zeros[:], rhs=zeros[:], start=True, stop=True)
+
+        warm(3)
 
         ident = keep.tile([P, P], F32, name="ident")
         make_identity(nc, ident[:])
@@ -78,17 +84,16 @@ def tile_quaternionlinear_kernel(tc, q_in, r_weight, i_weight, j_weight, k_weigh
             w_banks[d] = psum_o.tile([P, 4, P], F32, tag="o", name="w_bank%d" % d)
         w_grouped = {}
 
-        def transpose_weights():
+        def transpose_weights(d):
             for w in range(4):
-                for d in COMPONENTS:
-                    c = d ^ w
-                    nc.tensor.matmul(
-                        out=w_banks[d][:, c, :],
-                        lhsT=weights[w][:],
-                        rhs=plus[:] if SIGN[d][c] > 0 else minus[:],
-                        start=True,
-                        stop=True,
-                    )
+                c = d ^ w
+                nc.tensor.matmul(
+                    out=w_banks[d][:, c, :],
+                    lhsT=weights[w][:],
+                    rhs=plus[:] if SIGN[d][c] > 0 else minus[:],
+                    start=True,
+                    stop=True,
+                )
 
         def copy_weights(engine, d):
             wg = keep.tile([P, 4 * P], BF16, name="w_grouped%d" % d, align_bytes=64)
@@ -146,20 +151,21 @@ def tile_quaternionlinear_kernel(tc, q_in, r_weight, i_weight, j_weight, k_weigh
         def multiply(t):
             g, s = slot_of[t]
             acc = psum_o.tile([P, N_OUT], F32, tag="o", name="acc%d" % t)
-            nc.tensor.matmul_mx(
-                out=acc[:],
-                lhsT=q_codes[g][:, s * P : (s + 1) * P].bitcast(FP8X4),
-                lhsT_scale=q_scales[g][:, s * P : (s + 1) * P],
-                rhs=w_codes[:].bitcast(FP8X4),
-                rhs_scale=w_scales[:],
-                start=True,
-                stop=True,
-            )
+            for cols in (slice(N_OUT // 2, N_OUT), slice(0, N_OUT // 2)) if t == 0 else (slice(0, N_OUT),):
+                nc.tensor.matmul_mx(
+                    out=acc[:, cols],
+                    lhsT=q_codes[g][:, s * P : (s + 1) * P].bitcast(FP8X4),
+                    lhsT_scale=q_scales[g][:, s * P : (s + 1) * P],
+                    rhs=w_codes[:, cols].bitcast(FP8X4),
+                    rhs_scale=w_scales[:, cols],
+                    start=True,
+                    stop=True,
+                )
             si, ss = store_of[t]
             if si not in store_rows:
                 store_rows[si] = keep.tile([P, len(STORES[si]), N_OUT], F32, name="o_sb%d" % si)
             copy(
-                "V" if t >= TILES - 5 and t % 2 == 1 else "S",
+                "V" if t in VECTOR_TILES else "S",
                 store_rows[si][:, ss, :].rearrange("p (m d) -> p m d", d=4),
                 acc[:].rearrange("p (d m) -> p m d", d=4),
             )
@@ -168,21 +174,22 @@ def tile_quaternionlinear_kernel(tc, q_in, r_weight, i_weight, j_weight, k_weigh
                 t0 = STORES[si][0]
                 nc.sync.dma_start(out=out_view[:, t0 : t0 + len(STORES[si]), :], in_=store_rows[si][:])
 
-        transpose_weights()
-        transpose_tokens(0)
-        transpose_tokens(1)
+        for d in COMPONENTS:
+            transpose_weights(d)
+        for g in range(3):
+            transpose_tokens(g)
+            warm(1)
         copy_weights("V", 3)
         copy_weights("S", 2)
         copy_weights("V", 1)
         copy_weights("S", 0)
         copy_tokens("S", 0)
-        copy_tokens("S", 1)
         for d in COMPONENTS:
             quantise_weights(d)
+        copy_tokens("S", 1)
         quantise_tokens(0)
-        transpose_tokens(2)
-        copy_tokens("V", 2)
         quantise_tokens(1)
+        copy_tokens("V", 2)
         quantise_tokens(2)
         multiply(0)
         multiply(1)

@@ -16,12 +16,14 @@ N_OUT = 512
 TILES = TOKENS // P
 FLOPS = 2 * TOKENS * K * N_OUT
 
-SIGN = ((1, -1, -1, -1), (1, 1, 1, -1), (1, -1, 1, 1), (1, 1, -1, 1))
-COMPONENTS = (3, 2, 1, 0)
+PLANES = (
+    ((1, 1), (3, 1), (0, 1), (2, -1), (1, -1), (3, -1)),
+    ((3, 1), (1, -1), (2, 1), (0, 1), (3, -1), (1, 1)),
+)
 
 LOAD_CHUNKS = (1, 3, 4, 4, 6)
 GROUPS = ((0,), (1,)) + tuple((t, t + 1) for t in range(2, TILES, 2))
-VECTOR_TILES = (11, 15, 17)
+VECTOR_TILES = (11, 13, 15, 17)
 STORES = ((0,), (1,)) + tuple((t, t + 1) for t in range(2, TILES - 2, 2)) + ((TILES - 2,), (TILES - 1,))
 
 
@@ -38,31 +40,34 @@ def tile_quaternionlinear_kernel(tc, q_in, r_weight, i_weight, j_weight, k_weigh
 
     with ExitStack() as ctx:
         keep = ctx.enter_context(tc.tile_pool(name="keep", bufs=1))
-        psum_t = ctx.enter_context(tc.psum_pool(name="psum_t", bufs=3))
-        psum_w = ctx.enter_context(tc.psum_pool(name="psum_w", bufs=1))
+        psum_t = ctx.enter_context(tc.psum_pool(name="psum_t", bufs=4))
         psum_o = ctx.enter_context(tc.psum_pool(name="psum_o", bufs=4))
         ctx.enter_context(tc.manual_schedule())
 
+        q_tiles = []
+
+        def load_tokens(ci):
+            count = LOAD_CHUNKS[ci]
+            first = len(q_tiles)
+            q_chunk = keep.tile([P, count, K], BF16, name="q_chunk%d" % ci)
+            nc.sync.dma_start(out=q_chunk[:], in_=q_view[:, first : first + count, :])
+            for j in range(count):
+                q_tiles.append(q_chunk[:, j, :])
+
+        load_tokens(0)
         weights = []
         for name, weight in (("w_r", r_weight), ("w_i", i_weight), ("w_j", j_weight), ("w_k", k_weight)):
             w_sb = keep.tile([P, P], BF16, name=name)
             nc.sync.dma_start(out=w_sb[:], in_=weight)
             weights.append(w_sb)
-
-        q_tiles = []
-        first = 0
-        for ci, count in enumerate(LOAD_CHUNKS):
-            q_chunk = keep.tile([P, count, K], BF16, name="q_chunk%d" % ci)
-            nc.sync.dma_start(out=q_chunk[:], in_=q_view[:, first : first + count, :])
-            for j in range(count):
-                q_tiles.append(q_chunk[:, j, :])
-            first += count
+        for ci in range(1, len(LOAD_CHUNKS)):
+            load_tokens(ci)
 
         zeros = keep.tile([P, P], F32, name="zeros")
         nc.vector.memset(zeros[:], 0.0)
         scratch = keep.tile([P, 1], F32, name="scratch")
         nc.scalar.copy(out=scratch[:], in_=zeros[:, 0:1])
-        warm_bank = psum_w.tile([P, P], F32, name="warm_bank")
+        warm_bank = psum_o.tile([P, P], F32, tag="o", name="warm_bank")
 
         def warm(count):
             for r in range(count):
@@ -80,24 +85,24 @@ def tile_quaternionlinear_kernel(tc, q_in, r_weight, i_weight, j_weight, k_weigh
         w_codes = keep.tile([P, N_OUT], U32, name="w_codes", align_bytes=64)
         w_scales = keep.tile([P, N_OUT], U8, name="w_scales", align_bytes=64)
         w_banks = {}
-        for d in COMPONENTS:
-            w_banks[d] = psum_o.tile([P, 4, P], F32, tag="o", name="w_bank%d" % d)
         w_grouped = {}
 
-        def transpose_weights(d):
-            for w in range(4):
-                c = d ^ w
+        def transpose_weights(b):
+            w_bank = psum_o.tile([P, 6, P], BF16, tag="o", name="w_bank%d" % b)
+            for x, (w, sign) in enumerate(PLANES[b]):
                 nc.tensor.matmul(
-                    out=w_banks[d][:, c, :],
-                    lhsT=weights[w][:],
-                    rhs=plus[:] if SIGN[d][c] > 0 else minus[:],
-                    start=True,
-                    stop=True,
+                    out=w_bank[:, x, :], lhsT=weights[w][:], rhs=plus[:] if sign > 0 else minus[:], start=True, stop=True
                 )
+            w_banks[b] = w_bank
 
         def copy_weights(engine, d):
             wg = keep.tile([P, 4 * P], BF16, name="w_grouped%d" % d, align_bytes=64)
-            copy(engine, wg[:].rearrange("p (m c) -> p m c", c=4), w_banks[d][:].rearrange("p c m -> p m c"))
+            first = 0 if d % 2 == 1 else 2
+            copy(
+                engine,
+                wg[:].rearrange("p (m h e) -> p m h e", h=2, e=2),
+                w_banks[d // 2][:, first : first + 4, :].rearrange("p (e h) m -> p m h e", e=2),
+            )
             w_grouped[d] = wg
 
         def quantise_weights(d):
@@ -174,26 +179,37 @@ def tile_quaternionlinear_kernel(tc, q_in, r_weight, i_weight, j_weight, k_weigh
                 t0 = STORES[si][0]
                 nc.sync.dma_start(out=out_view[:, t0 : t0 + len(STORES[si]), :], in_=store_rows[si][:])
 
-        for d in COMPONENTS:
-            transpose_weights(d)
-        for g in range(3):
-            transpose_tokens(g)
-            warm(1)
-        copy_weights("V", 3)
-        copy_weights("S", 2)
-        copy_weights("V", 1)
-        copy_weights("S", 0)
+        transpose_tokens(0)
+        transpose_weights(1)
+        transpose_weights(0)
+        transpose_tokens(1)
+        transpose_tokens(2)
+        warm(1)
+        transpose_tokens(3)
         copy_tokens("S", 0)
-        for d in COMPONENTS:
-            quantise_weights(d)
-        copy_tokens("S", 1)
+        copy_weights("V", 3)
         quantise_tokens(0)
+        copy_weights("V", 2)
+        copy_weights("S", 1)
+        copy_weights("S", 0)
+        quantise_weights(3)
+        quantise_weights(1)
+        quantise_weights(2)
+        copy_tokens("S", 1)
+        copy_tokens("S", 2)
+        quantise_weights(0)
         quantise_tokens(1)
-        copy_tokens("V", 2)
+        copy_tokens("V", 3)
         quantise_tokens(2)
+        quantise_tokens(3)
         multiply(0)
         multiply(1)
-        for prepared, multiplied in (((3, 4), (2,)), ((5, 6), (3, 4)), ((7, 8), (5, 6)), ((9,), (7, 8, 9))):
+        transpose_tokens(4)
+        copy_tokens("V", 4)
+        multiply(2)
+        multiply(3)
+        quantise_tokens(4)
+        for prepared, multiplied in (((5, 6), (3, 4)), ((7, 8), (5, 6)), ((9,), (7, 8, 9))):
             for g in prepared:
                 transpose_tokens(g)
             for g in prepared:

@@ -24,7 +24,7 @@ PLANES = (
 LOAD_CHUNKS = (1, 3, 4, 4, 6)
 GROUPS = ((0,), (1,)) + tuple((t, t + 1) for t in range(2, TILES, 2))
 VECTOR_TILES = (11, 13, 15, 17)
-STORES = ((0,), (1,)) + tuple((t, t + 1) for t in range(2, TILES - 2, 2)) + ((TILES - 2,), (TILES - 1,))
+STORES = tuple((t,) for t in range(TILES))
 
 
 def tile_quaternionlinear_kernel(tc, q_in, r_weight, i_weight, j_weight, k_weight, out):

@@ -24,7 +24,7 @@ PLANES = (
 LOAD_CHUNKS = (1, 3, 4, 4, 6)
 GROUPS = ((0,), (1,)) + tuple((t, t + 1) for t in range(2, TILES, 2))
 VECTOR_TILES = (11, 13, 15, 17)
-STORES = tuple((t,) for t in range(TILES))
+STORES = tuple((t,) for t in range(6)) + tuple((t, t + 1) for t in range(6, TILES - 2, 2)) + ((TILES - 2,), (TILES - 1,))
 
 
 def tile_quaternionlinear_kernel(tc, q_in, r_weight, i_weight, j_weight, k_weight, out):
@@ -183,6 +183,7 @@ def tile_quaternionlinear_kernel(tc, q_in, r_weight, i_weight, j_weight, k_weigh
         transpose_weights(1)
         transpose_weights(0)
         transpose_tokens(1)
+        warm(1)
         transpose_tokens(2)
         warm(1)
         transpose_tokens(3)

from contextlib import ExitStack

import concourse.mybir as mybir
from concourse.masks import make_identity

F32 = mybir.dt.float32
BF16 = mybir.dt.bfloat16
U32 = mybir.dt.uint32
U8 = mybir.dt.uint8
FP8X4 = mybir.dt.float8_e4m3fn_x4

P = 128
TOKENS = 4 * 576
K = 512
N_OUT = 512
TILES = TOKENS // P
FLOPS = 2 * TOKENS * K * N_OUT

PLANES = (
    ((1, 1), (3, 1), (0, 1), (2, -1), (1, -1), (3, -1)),
    ((3, 1), (1, -1), (2, 1), (0, 1), (3, -1), (1, 1)),
)

LOAD_CHUNKS = (1, 3, 4, 4, 6)
GROUPS = ((0,), (1,)) + tuple((t, t + 1) for t in range(2, TILES, 2))
VECTOR_TILES = (11, 13, 15, 17)
STORES = tuple((t,) for t in range(6)) + tuple((t, t + 1) for t in range(6, TILES - 2, 2)) + ((TILES - 2,), (TILES - 1,))


def tile_quaternionlinear_kernel(tc, q_in, r_weight, i_weight, j_weight, k_weight, out):
    nc = tc.nc
    q_view = q_in.flatten_outer_dims().rearrange("(p t) k -> p t k", t=TILES)
    out_view = out.flatten_outer_dims().rearrange("(p t) c -> p t c", t=TILES)

    def copy(engine, dst, src):
        if engine == "V":
            nc.vector.tensor_copy(out=dst, in_=src)
        else:
            nc.scalar.copy(out=dst, in_=src)

    with ExitStack() as ctx:
        keep = ctx.enter_context(tc.tile_pool(name="keep", bufs=1))
        psum_t = ctx.enter_context(tc.psum_pool(name="psum_t", bufs=4))
        psum_o = ctx.enter_context(tc.psum_pool(name="psum_o", bufs=4))
        ctx.enter_context(tc.manual_schedule())

        q_tiles = []

        def load_tokens(ci):
            count = LOAD_CHUNKS[ci]
            first = len(q_tiles)
            q_chunk = keep.tile([P, count, K], BF16, name="q_chunk%d" % ci)
            nc.sync.dma_start(out=q_chunk[:], in_=q_view[:, first : first + count, :])
            for j in range(count):
                q_tiles.append(q_chunk[:, j, :])

        load_tokens(0)
        weights = []
        for name, weight in (("w_r", r_weight), ("w_i", i_weight), ("w_j", j_weight), ("w_k", k_weight)):
            w_sb = keep.tile([P, P], BF16, name=name)
            nc.sync.dma_start(out=w_sb[:], in_=weight)
            weights.append(w_sb)
        for ci in range(1, len(LOAD_CHUNKS)):
            load_tokens(ci)

        zeros = keep.tile([P, P], F32, name="zeros")
        nc.vector.memset(zeros[:], 0.0)
        scratch = keep.tile([P, 1], F32, name="scratch")
        nc.scalar.copy(out=scratch[:], in_=zeros[:, 0:1])
        warm_bank = psum_o.tile([P, P], F32, tag="o", name="warm_bank")

        def warm(count):
            for r in range(count):
                nc.tensor.matmul(out=warm_bank[:], lhsT=zeros[:], rhs=zeros[:], start=True, stop=True)

        warm(3)

        ident = keep.tile([P, P], F32, name="ident")
        make_identity(nc, ident[:])
        plus = keep.tile([P, P], BF16, name="plus")
        minus = keep.tile([P, P], BF16, name="minus")
        nc.vector.tensor_copy(out=plus[:], in_=ident[:])
        nc.vector.tensor_scalar_mul(out=minus[:], in0=ident[:], scalar1=-1.0)

        w_codes = keep.tile([P, N_OUT], U32, name="w_codes", align_bytes=64)
        w_scales = keep.tile([P, N_OUT], U8, name="w_scales", align_bytes=64)
        w_banks = {}
        w_grouped = {}

        def transpose_weights(b):
            w_bank = psum_o.tile([P, 6, P], BF16, tag="o", name="w_bank%d" % b)
            for x, (w, sign) in enumerate(PLANES[b]):
                nc.tensor.matmul(
                    out=w_bank[:, x, :], lhsT=weights[w][:], rhs=plus[:] if sign > 0 else minus[:], start=True, stop=True
                )
            w_banks[b] = w_bank

        def copy_weights(engine, d):
            wg = keep.tile([P, 4 * P], BF16, name="w_grouped%d" % d, align_bytes=64)
            first = 0 if d % 2 == 1 else 2
            copy(
                engine,
                wg[:].rearrange("p (m h e) -> p m h e", h=2, e=2),
                w_banks[d // 2][:, first : first + 4, :].rearrange("p (e h) m -> p m h e", e=2),
            )
            w_grouped[d] = wg

        def quantise_weights(d):
            cols = slice(d * P, (d + 1) * P)
            nc.vector.quantize_mx(out=w_codes[:, cols].bitcast(FP8X4), scales=w_scales[:, cols], in_=w_grouped[d][:])

        q_banks = {}
        q_grouped = {}
        q_codes = {}
        q_scales = {}
        slot_of = {}
        for g, tiles in enumerate(GROUPS):
            for s, t in enumerate(tiles):
                slot_of[t] = (g, s)

        def transpose_tokens(g):
            count = len(GROUPS[g])
            tq = psum_t.tile([P, count, 2, P], F32, tag="t", name="tq%d" % g)
            for s, t in enumerate(GROUPS[g]):
                words = q_tiles[t].bitcast(F32)
                for u in range(2):
                    nc.tensor.transpose(tq[:, s, u, :], words[:, u : 2 * P : 2], ident[:])
            q_banks[g] = tq

        def copy_tokens(engine, g):
            count = len(GROUPS[g])
            grouped = keep.tile([P, count * 4 * P], BF16, name="grouped%d" % g, align_bytes=64)
            copy(
                engine,
                grouped[:].bitcast(F32).rearrange("p (s k u) -> p s k u", s=count, u=2),
                q_banks[g][:].rearrange("p s u k -> p s k u"),
            )
            q_grouped[g] = grouped

        def quantise_tokens(g):
            count = len(GROUPS[g])
            codes = keep.tile([P, count * P], U32, name="codes%d" % g, align_bytes=64)
            scales = keep.tile([P, count * P], U8, name="scales%d" % g, align_bytes=64)
            nc.vector.quantize_mx(out=codes[:].bitcast(FP8X4), scales=scales[:], in_=q_grouped[g][:])
            q_codes[g] = codes
            q_scales[g] = scales

        store_of = {}
        store_rows = {}
        left = {}
        for si, tiles in enumerate(STORES):
            left[si] = len(tiles)
            for s, t in enumerate(tiles):
                store_of[t] = (si, s)

        def multiply(t):
            g, s = slot_of[t]
            acc = psum_o.tile([P, N_OUT], F32, tag="o", name="acc%d" % t)
            for cols in (slice(N_OUT // 2, N_OUT), slice(0, N_OUT // 2)) if t == 0 else (slice(0, N_OUT),):
                nc.tensor.matmul_mx(
                    out=acc[:, cols],
                    lhsT=q_codes[g][:, s * P : (s + 1) * P].bitcast(FP8X4),
                    lhsT_scale=q_scales[g][:, s * P : (s + 1) * P],
                    rhs=w_codes[:, cols].bitcast(FP8X4),
                    rhs_scale=w_scales[:, cols],
                    start=True,
                    stop=True,
                )
            si, ss = store_of[t]
            if si not in store_rows:
                store_rows[si] = keep.tile([P, len(STORES[si]), N_OUT], F32, name="o_sb%d" % si)
            copy(
                "V" if t in VECTOR_TILES else "S",
                store_rows[si][:, ss, :].rearrange("p (m d) -> p m d", d=4),
                acc[:].rearrange("p (d m) -> p m d", d=4),
            )
            left[si] -= 1
            if left[si] == 0:
                t0 = STORES[si][0]
                nc.sync.dma_start(out=out_view[:, t0 : t0 + len(STORES[si]), :], in_=store_rows[si][:])

        transpose_tokens(0)
        transpose_weights(1)
        transpose_weights(0)
        transpose_tokens(1)
        warm(1)
        transpose_tokens(2)
        warm(1)
        transpose_tokens(3)
        copy_tokens("S", 0)
        copy_weights("V", 3)
        quantise_tokens(0)
        copy_weights("V", 2)
        copy_weights("S", 1)
        copy_weights("S", 0)
        quantise_weights(3)
        quantise_weights(1)
        quantise_weights(2)
        copy_tokens("S", 1)
        copy_tokens("S", 2)
        quantise_weights(0)
        quantise_tokens(1)
        copy_tokens("V", 3)
        quantise_tokens(2)
        quantise_tokens(3)
        multiply(0)
        multiply(1)
        transpose_tokens(4)
        copy_tokens("V", 4)
        multiply(2)
        multiply(3)
        quantise_tokens(4)
        for prepared, multiplied in (((5, 6), (3, 4)), ((7, 8), (5, 6)), ((9,), (7, 8, 9))):
            for g in prepared:
                transpose_tokens(g)
            for g in prepared:
                copy_tokens("V", g)
            for g in prepared:
                quantise_tokens(g)
            for g in multiplied:
                for t in GROUPS[g]:
                    multiply(t)
